import numpy as np
import ml_dtypes


def mxq(x, axis, fmt="e4m3"):
    dtype, down = {"e4m3": (ml_dtypes.float8_e4m3fn, 7), "e5m2": (ml_dtypes.float8_e5m2, 14)}[fmt]
    v = np.moveaxis(np.asarray(x, np.float32).astype(ml_dtypes.bfloat16).astype(np.float64), axis, -1)
    blocks = v.reshape(v.shape[:-1] + (-1, 32))
    amax = np.abs(blocks).max(-1, keepdims=True)
    byte = np.maximum(np.where(amax > 0, np.frexp(amax)[1] - 1 + 127, 0) - down, 1)
    scale = np.exp2(byte - 127.0)
    codes = (blocks / scale).astype(np.float32).astype(dtype).astype(np.float64)
    return np.moveaxis((codes * scale).reshape(v.shape), -1, axis)


WIDE = False


def mx_kscale(k):
    if not WIDE:
        return np.ones(k)
    levels = np.array([10, -10, 5, -5, 0])
    a = np.random.permutation(np.resize(levels, k // 512 * 4)).reshape(k // 512, 4)
    idx = np.arange(k)
    return np.exp2(a[idx // 512, idx % 128 // 32])


BF16 = ml_dtypes.bfloat16


def bf(x):
    return np.asarray(x, np.float32).astype(BF16)


def f64(x):
    return np.asarray(x).astype(np.float64)


B, CB, CD, H, W = 4, 2, 512, 32, 32
C = CB * CD


def erf(z):
    z = np.clip(z, -6.0, 6.0)
    z2 = 2.0 * z * z
    term = z.copy()
    tot = z.copy()
    for n in range(1, 101):
        term *= z2
        term /= 2 * n + 1
        tot += term
    return 2.0 / np.sqrt(np.pi) * np.exp(-z * z) * tot


def gelu_erf(v):
    return 0.5 * v * (1.0 + erf(v / np.sqrt(2.0)))


def setup_inputs():
    s = mx_kscale(CD)
    s = s / s.max()
    sc = np.tile(s, CB)
    return {"x": bf(np.random.standard_normal((B, C, H, W)) * sc[None, :, None, None]),
            "wc": bf(np.random.standard_normal((CB, CD, CD)) / np.sqrt(CD) / s[None, :, None])}


def reference(x, wc):
    x = f64(x)
    xr = np.transpose(x, (0, 2, 3, 1)).reshape(B, H, W, CB, CD)
    xb = xr.transpose(3, 0, 1, 2, 4).reshape(CB, B * H * W, CD)
    out = mxq(xb, 2, "e4m3") @ mxq(f64(wc), 1, "e4m3")
    out = out.reshape(CB, B, H, W, CD).transpose(1, 2, 3, 0, 4)
    out = out.reshape(B, H, W, C).transpose(0, 3, 1, 2)
    return gelu_erf(x + out)

@@ -1,0 +1,175 @@
+from contextlib import ExitStack
+
+import concourse.mybir as mybir
+
+FLOPS = 2 * 4 * 1024 * 2 * 512 * 512
+
+BF16 = mybir.dt.bfloat16
+F32 = mybir.dt.float32
+U32 = mybir.dt.uint32
+U8 = mybir.dt.uint8
+FP8X4 = mybir.dt.float8_e4m3fn_x4
+ADD = mybir.AluOpType.add
+MULT = mybir.AluOpType.mult
+GELU = mybir.ActivationFunctionType.Gelu
+
+P = 128
+PACK = 4
+HW = 1024
+HALF = 512
+NB = 4
+NI = 2
+NG = NB * NI
+GC = 768
+QPOS = 5
+NSUM = 5
+
+
+def tile_spectralchannelmixing_t_kernel(tc, x, wc, out):
+    nc = tc.nc
+    x_v = x.rearrange("b (i p t) h w -> b i p t (h w)", i=NI, p=P, t=PACK)
+    o_v = out.rearrange("b (i q m) h w -> b i q m (h w)", i=NI, q=P, m=PACK)
+    w_v = wc.rearrange("i (p t) k -> i p t k", t=PACK)
+
+    with ExitStack() as ctx:
+        keep = ctx.enter_context(tc.tile_pool(name="keep", bufs=1))
+        qx = ctx.enter_context(tc.tile_pool(name="qx", bufs=2))
+        sums = ctx.enter_context(tc.tile_pool(name="sums", bufs=NSUM))
+        psum = ctx.enter_context(tc.psum_pool(name="psum", bufs=8))
+        ctx.enter_context(tc.manual_schedule())
+
+        def bi(g):
+            return g % NB, g // NB
+
+        warm = keep.tile([P, 1], F32, name="warm")
+        nc.vector.memset(warm[:], 0.0)
+        nc.scalar.activation(out=warm[:], in_=warm[:], func=GELU)
+
+        w_raw = [keep.tile([P, PACK, 512], BF16, name="w_raw%d" % i) for i in range(NI)]
+        xs = [keep.tile([P, PACK, HW], BF16, name="xs%d" % g) for g in range(NG)]
+        nc.sync.dma_start(out=w_raw[0][:], in_=w_v[0])
+        nc.sync.dma_start(out=xs[0][:, :, 0:HALF], in_=x_v[0, 0][:, :, 0:HALF])
+        nc.sync.dma_start(out=xs[0][:, :, HALF:HW], in_=x_v[0, 0][:, :, HALF:HW])
+        nc.sync.dma_start(out=w_raw[1][:], in_=w_v[1])
+        for g in range(1, NG):
+            b, i = bi(g)
+            nc.sync.dma_start(out=xs[g][:], in_=x_v[b, i])
+
+        w_grp = [keep.tile([P, PACK, P, PACK], BF16, name="w_grp%d" % i, align_bytes=64) for i in range(NI)]
+        w_codes = [keep.tile([P, 512], U32, name="w_codes%d" % i, align_bytes=64) for i in range(NI)]
+        w_scales = [keep.tile([P, 512], U8, name="w_scales%d" % i, align_bytes=64) for i in range(NI)]
+        g_big = keep.tile([P, GC, PACK], BF16, name="g_big", align_bytes=64)
+        g_small = [keep.tile([P, HW - GC, PACK], BF16, name="g_small%d" % k, align_bytes=64) for k in range(2)]
+        codes = {}
+        scales = {}
+
+        def region(g, c0, c1):
+            if c1 <= GC:
+                return g_big[:, c0:c1, :]
+            return g_small[g % 2][:, c0 - GC : c1 - GC, :]
+
+        def regroup(g, plan):
+            for eng, c0, c1 in plan:
+                dst = region(g, c0, c1)
+                if eng == "G":
+                    nc.gpsimd.tensor_scalar(
+                        out=dst,
+                        in0=xs[g][:, :, c0:c1].rearrange("p t w -> p w t"),
+                        scalar1=1.0,
+                        scalar2=0.0,
+                        op0=MULT,
+                        op1=ADD,
+                    )
+                else:
+                    d4 = dst.rearrange("p (c i) t -> p c t i", i=4)
+                    s4 = xs[g][:, :, c0:c1].rearrange("p t (c i) -> p c t i", i=4)
+                    if eng == "V":
+                        nc.vector.tensor_copy(out=d4, in_=s4)
+                    else:
+                        nc.scalar.copy(out=d4, in_=s4)
+
+        def quant(g, calls):
+            if g not in codes:
+                codes[g] = qx.tile([P, HW], U32, name="codes", align_bytes=64)
+                scales[g] = qx.tile([P, HW], U8, name="scales", align_bytes=64)
+            for c0, c1 in calls:
+                nc.vector.quantize_mx(
+                    out=codes[g][:, c0:c1].bitcast(FP8X4),
+                    scales=scales[g][:, c0:c1],
+                    in_=region(g, c0, c1).rearrange("p w t -> p (w t)"),
+                )
+
+        def w_regroup(i, eng):
+            src = w_raw[i][:].rearrange("p t (q m) -> p m q t", m=PACK)
+            if eng == "V":
+                nc.vector.tensor_copy(out=w_grp[i][:], in_=src)
+            else:
+                nc.scalar.copy(out=w_grp[i][:], in_=src)
+
+        def w_quant(i):
+            nc.vector.quantize_mx(
+                out=w_codes[i][:].bitcast(FP8X4),
+                scales=w_scales[i][:],
+                in_=w_grp[i][:].rearrange("p m q t -> p (m q t)"),
+            )
+
+        steady_plan = [("G", 0, GC), ("S", GC, HW)]
+        steady_calls = [(GC, HW), (0, HALF), (HALF, GC)]
+
+        w_regroup(0, "V")
+        regroup(0, [("S", 0, 256), ("V", 256, HALF)])
+        w_quant(0)
+        quant(0, [(0, HALF)])
+        regroup(0, [("G", HALF, GC), ("S", GC, HW)])
+        w_regroup(1, "S")
+
+        for g in range(NG):
+            b, i = bi(g)
+            s = sums.tile([P, PACK, HW], F32, name="s")
+            if g == 0:
+                order = [(m, h) for h in range(2) for m in range(PACK)]
+            else:
+                order = [(m, h) for m in range(PACK) for h in range(2)]
+            for n, (m, h) in enumerate(order):
+                cols = slice(h * HALF, (h + 1) * HALF)
+                acc = psum.tile([P, HALF], F32, name="acc")
+                nc.tensor.matmul_mx(
+                    out=acc[:],
+                    lhsT=w_codes[i][:, m * P : (m + 1) * P].bitcast(FP8X4),
+                    lhsT_scale=w_scales[i][:, m * P : (m + 1) * P],
+                    rhs=codes[g][:, cols].bitcast(FP8X4),
+                    rhs_scale=scales[g][:, cols],
+                    start=True,
+                    stop=True,
+                )
+                nc.vector.tensor_tensor(out=s[:, m, cols], in0=acc[:], in1=xs[g][:, m, cols], op=ADD)
+                if g == 0:
+                    if m == PACK - 1:
+                        nc.scalar.activation(out=s[:, :, cols], in_=s[:, :, cols], func=GELU)
+                        if h == 1:
+                            nc.sync.dma_start(out=o_v[b, i], in_=s[:])
+                elif g < NG - 1:
+                    if h == 1:
+                        nc.scalar.activation(out=s[:, m, :], in_=s[:, m, :], func=GELU)
+                        if m % 2 == 1:
+                            nc.sync.dma_start(out=o_v[b, i][:, m - 1 : m + 1, :], in_=s[:, m - 1 : m + 1, :])
+                elif m < PACK - 1:
+                    if h == 1:
+                        nc.scalar.activation(out=s[:, m, :], in_=s[:, m, :], func=GELU)
+                        nc.sync.dma_start(out=o_v[b, i][:, m, :], in_=s[:, m, :])
+                else:
+                    nc.scalar.activation(out=s[:, m, cols], in_=s[:, m, cols], func=GELU)
+                    nc.sync.dma_start(out=o_v[b, i][:, m, cols], in_=s[:, m, cols])
+
+                if g == 0 and n == 1:
+                    quant(0, [(GC, HW), (HALF, GC)])
+                    regroup(1, [("G", 0, HALF), ("S", HALF, GC), ("S", GC, HW)])
+                elif g == 0 and n == 5:
+                    w_quant(1)
+                    quant(1, steady_calls)
+                    regroup(2, steady_plan)
+                elif g >= 1 and n == QPOS:
+                    if g + 1 < NG:
+                        quant(g + 1, steady_calls)
+                    if g + 2 < NG:
+                        regroup(g + 2, steady_plan)

@@ -23,6 +23,7 @@ NG = NB * NI
 GC = 768
 QPOS = 5
 NSUM = 5
+FINE = 5
 
 
 def tile_spectralchannelmixing_t_kernel(tc, x, wc, out):
@@ -50,10 +51,11 @@ def tile_spectralchannelmixing_t_kernel(tc, x, wc, out):
         nc.sync.dma_start(out=w_raw[0][:], in_=w_v[0])
         nc.sync.dma_start(out=xs[0][:, :, 0:HALF], in_=x_v[0, 0][:, :, 0:HALF])
         nc.sync.dma_start(out=xs[0][:, :, HALF:HW], in_=x_v[0, 0][:, :, HALF:HW])
-        nc.sync.dma_start(out=w_raw[1][:], in_=w_v[1])
         for g in range(1, NG):
             b, i = bi(g)
             nc.sync.dma_start(out=xs[g][:], in_=x_v[b, i])
+            if g == 1:
+                nc.sync.dma_start(out=w_raw[1][:], in_=w_v[1])
 
         w_grp = [keep.tile([P, PACK, P, PACK], BF16, name="w_grp%d" % i, align_bytes=64) for i in range(NI)]
         w_codes = [keep.tile([P, 512], U32, name="w_codes%d" % i, align_bytes=64) for i in range(NI)]
@@ -120,8 +122,9 @@ def tile_spectralchannelmixing_t_kernel(tc, x, wc, out):
         regroup(0, [("S", 0, 256), ("V", 256, HALF)])
         w_quant(0)
         quant(0, [(0, HALF)])
-        regroup(0, [("G", HALF, GC), ("S", GC, HW)])
-        w_regroup(1, "S")
+        regroup(0, [("S", GC, HW), ("V", HALF, GC)])
+        quant(0, [(GC, HW), (HALF, GC)])
+        regroup(1, [("G", 0, HALF), ("S", HALF, GC), ("S", GC, HW)])
 
         for g in range(NG):
             b, i = bi(g)
@@ -148,12 +151,12 @@ def tile_spectralchannelmixing_t_kernel(tc, x, wc, out):
                         nc.scalar.activation(out=s[:, :, cols], in_=s[:, :, cols], func=GELU)
                         if h == 1:
                             nc.sync.dma_start(out=o_v[b, i], in_=s[:])
-                elif g < NG - 1:
+                elif g < FINE:
                     if h == 1:
                         nc.scalar.activation(out=s[:, m, :], in_=s[:, m, :], func=GELU)
                         if m % 2 == 1:
                             nc.sync.dma_start(out=o_v[b, i][:, m - 1 : m + 1, :], in_=s[:, m - 1 : m + 1, :])
-                elif m < PACK - 1:
+                elif g < NG - 1 or m < PACK - 1:
                     if h == 1:
                         nc.scalar.activation(out=s[:, m, :], in_=s[:, m, :], func=GELU)
                         nc.sync.dma_start(out=o_v[b, i][:, m, :], in_=s[:, m, :])
@@ -161,15 +164,12 @@ def tile_spectralchannelmixing_t_kernel(tc, x, wc, out):
                     nc.scalar.activation(out=s[:, m, cols], in_=s[:, m, cols], func=GELU)
                     nc.sync.dma_start(out=o_v[b, i][:, m, cols], in_=s[:, m, cols])
 
-                if g == 0 and n == 1:
-                    quant(0, [(GC, HW), (HALF, GC)])
-                    regroup(1, [("G", 0, HALF), ("S", HALF, GC), ("S", GC, HW)])
-                elif g == 0 and n == 5:
-                    w_quant(1)
-                    quant(1, steady_calls)
-                    regroup(2, steady_plan)
-                elif g >= 1 and n == QPOS:
+                if n == QPOS:
+                    if g == 1:
+                        w_quant(1)
                     if g + 1 < NG:
                         quant(g + 1, steady_calls)
                     if g + 2 < NG:
                         regroup(g + 2, steady_plan)
+                    if g == 0:
+                        w_regroup(1, "S")

@@ -20,10 +20,9 @@ HALF = 512
 NB = 4
 NI = 2
 NG = NB * NI
-GC = 768
+GC = 832
 QPOS = 5
 NSUM = 5
-FINE = 5
 
 
 def tile_spectralchannelmixing_t_kernel(tc, x, wc, out):
@@ -51,11 +50,10 @@ def tile_spectralchannelmixing_t_kernel(tc, x, wc, out):
         nc.sync.dma_start(out=w_raw[0][:], in_=w_v[0])
         nc.sync.dma_start(out=xs[0][:, :, 0:HALF], in_=x_v[0, 0][:, :, 0:HALF])
         nc.sync.dma_start(out=xs[0][:, :, HALF:HW], in_=x_v[0, 0][:, :, HALF:HW])
+        nc.sync.dma_start(out=w_raw[1][:], in_=w_v[1])
         for g in range(1, NG):
             b, i = bi(g)
             nc.sync.dma_start(out=xs[g][:], in_=x_v[b, i])
-            if g == 1:
-                nc.sync.dma_start(out=w_raw[1][:], in_=w_v[1])
 
         w_grp = [keep.tile([P, PACK, P, PACK], BF16, name="w_grp%d" % i, align_bytes=64) for i in range(NI)]
         w_codes = [keep.tile([P, 512], U32, name="w_codes%d" % i, align_bytes=64) for i in range(NI)]
@@ -90,11 +88,22 @@ def tile_spectralchannelmixing_t_kernel(tc, x, wc, out):
                     else:
                         nc.scalar.copy(out=d4, in_=s4)
 
+        def pieces(c0, c1):
+            cuts = []
+            c = c0
+            while c < c1:
+                w = HW
+                while w > c1 - c or c % w:
+                    w //= 2
+                cuts.append((c, c + w))
+                c += w
+            return cuts
+
         def quant(g, calls):
             if g not in codes:
                 codes[g] = qx.tile([P, HW], U32, name="codes", align_bytes=64)
                 scales[g] = qx.tile([P, HW], U8, name="scales", align_bytes=64)
-            for c0, c1 in calls:
+            for c0, c1 in [pc for rng in calls for pc in pieces(rng[0], rng[1])]:
                 nc.vector.quantize_mx(
                     out=codes[g][:, c0:c1].bitcast(FP8X4),
                     scales=scales[g][:, c0:c1],
@@ -116,15 +125,14 @@ def tile_spectralchannelmixing_t_kernel(tc, x, wc, out):
             )
 
         steady_plan = [("G", 0, GC), ("S", GC, HW)]
-        steady_calls = [(GC, HW), (0, HALF), (HALF, GC)]
+        steady_calls = [(GC, HW), (0, GC)]
 
         w_regroup(0, "V")
         regroup(0, [("S", 0, 256), ("V", 256, HALF)])
         w_quant(0)
         quant(0, [(0, HALF)])
-        regroup(0, [("S", GC, HW), ("V", HALF, GC)])
-        quant(0, [(GC, HW), (HALF, GC)])
-        regroup(1, [("G", 0, HALF), ("S", HALF, GC), ("S", GC, HW)])
+        regroup(0, [("G", HALF, GC), ("S", GC, HW)])
+        w_regroup(1, "S")
 
         for g in range(NG):
             b, i = bi(g)
@@ -151,12 +159,12 @@ def tile_spectralchannelmixing_t_kernel(tc, x, wc, out):
                         nc.scalar.activation(out=s[:, :, cols], in_=s[:, :, cols], func=GELU)
                         if h == 1:
                             nc.sync.dma_start(out=o_v[b, i], in_=s[:])
-                elif g < FINE:
+                elif g < NG - 1:
                     if h == 1:
                         nc.scalar.activation(out=s[:, m, :], in_=s[:, m, :], func=GELU)
                         if m % 2 == 1:
                             nc.sync.dma_start(out=o_v[b, i][:, m - 1 : m + 1, :], in_=s[:, m - 1 : m + 1, :])
-                elif g < NG - 1 or m < PACK - 1:
+                elif m < PACK - 1:
                     if h == 1:
                         nc.scalar.activation(out=s[:, m, :], in_=s[:, m, :], func=GELU)
                         nc.sync.dma_start(out=o_v[b, i][:, m, :], in_=s[:, m, :])
@@ -164,12 +172,15 @@ def tile_spectralchannelmixing_t_kernel(tc, x, wc, out):
                     nc.scalar.activation(out=s[:, m, cols], in_=s[:, m, cols], func=GELU)
                     nc.sync.dma_start(out=o_v[b, i][:, m, cols], in_=s[:, m, cols])
 
-                if n == QPOS:
-                    if g == 1:
-                        w_quant(1)
+                if g == 0 and n == 1:
+                    quant(0, [(GC, HW), (HALF, GC)])
+                    regroup(1, [("G", 0, HALF), ("S", HALF, GC), ("S", GC, HW)])
+                elif g == 0 and n == 5:
+                    w_quant(1)
+                    quant(1, steady_calls)
+                    regroup(2, steady_plan)
+                elif g >= 1 and n == QPOS:
                     if g + 1 < NG:
                         quant(g + 1, steady_calls)
                     if g + 2 < NG:
                         regroup(g + 2, steady_plan)
-                    if g == 0:
-                        w_regroup(1, "S")

@@ -20,9 +20,11 @@ HALF = 512
 NB = 4
 NI = 2
 NG = NB * NI
-GC = 832
+GC = 768
 QPOS = 5
 NSUM = 5
+WHOLE = 3
+FINE = 5
 
 
 def tile_spectralchannelmixing_t_kernel(tc, x, wc, out):
@@ -88,22 +90,11 @@ def tile_spectralchannelmixing_t_kernel(tc, x, wc, out):
                     else:
                         nc.scalar.copy(out=d4, in_=s4)
 
-        def pieces(c0, c1):
-            cuts = []
-            c = c0
-            while c < c1:
-                w = HW
-                while w > c1 - c or c % w:
-                    w //= 2
-                cuts.append((c, c + w))
-                c += w
-            return cuts
-
         def quant(g, calls):
             if g not in codes:
                 codes[g] = qx.tile([P, HW], U32, name="codes", align_bytes=64)
                 scales[g] = qx.tile([P, HW], U8, name="scales", align_bytes=64)
-            for c0, c1 in [pc for rng in calls for pc in pieces(rng[0], rng[1])]:
+            for c0, c1 in calls:
                 nc.vector.quantize_mx(
                     out=codes[g][:, c0:c1].bitcast(FP8X4),
                     scales=scales[g][:, c0:c1],
@@ -125,7 +116,7 @@ def tile_spectralchannelmixing_t_kernel(tc, x, wc, out):
             )
 
         steady_plan = [("G", 0, GC), ("S", GC, HW)]
-        steady_calls = [(GC, HW), (0, GC)]
+        steady_calls = [(GC, HW), (0, HALF), (HALF, GC)]
 
         w_regroup(0, "V")
         regroup(0, [("S", 0, 256), ("V", 256, HALF)])
@@ -159,12 +150,15 @@ def tile_spectralchannelmixing_t_kernel(tc, x, wc, out):
                         nc.scalar.activation(out=s[:, :, cols], in_=s[:, :, cols], func=GELU)
                         if h == 1:
                             nc.sync.dma_start(out=o_v[b, i], in_=s[:])
-                elif g < NG - 1:
+                elif g < FINE:
                     if h == 1:
                         nc.scalar.activation(out=s[:, m, :], in_=s[:, m, :], func=GELU)
-                        if m % 2 == 1:
+                        if g < WHOLE:
+                            if m == PACK - 1:
+                                nc.sync.dma_start(out=o_v[b, i], in_=s[:])
+                        elif m % 2 == 1:
                             nc.sync.dma_start(out=o_v[b, i][:, m - 1 : m + 1, :], in_=s[:, m - 1 : m + 1, :])
-                elif m < PACK - 1:
+                elif g < NG - 1 or m < PACK - 1:
                     if h == 1:
                         nc.scalar.activation(out=s[:, m, :], in_=s[:, m, :], func=GELU)
                         nc.sync.dma_start(out=o_v[b, i][:, m, :], in_=s[:, m, :])

@@ -20,11 +20,9 @@ HALF = 512
 NB = 4
 NI = 2
 NG = NB * NI
-GC = 768
+SC = 256
 QPOS = 5
 NSUM = 5
-WHOLE = 3
-FINE = 5
 
 
 def tile_spectralchannelmixing_t_kernel(tc, x, wc, out):
@@ -60,15 +58,13 @@ def tile_spectralchannelmixing_t_kernel(tc, x, wc, out):
         w_grp = [keep.tile([P, PACK, P, PACK], BF16, name="w_grp%d" % i, align_bytes=64) for i in range(NI)]
         w_codes = [keep.tile([P, 512], U32, name="w_codes%d" % i, align_bytes=64) for i in range(NI)]
         w_scales = [keep.tile([P, 512], U8, name="w_scales%d" % i, align_bytes=64) for i in range(NI)]
-        g_big = keep.tile([P, GC, PACK], BF16, name="g_big", align_bytes=64)
-        g_small = [keep.tile([P, HW - GC, PACK], BF16, name="g_small%d" % k, align_bytes=64) for k in range(2)]
+        grp = keep.tile([P, HW + SC, PACK], BF16, name="grp", align_bytes=64)
         codes = {}
         scales = {}
 
         def region(g, c0, c1):
-            if c1 <= GC:
-                return g_big[:, c0:c1, :]
-            return g_small[g % 2][:, c0 - GC : c1 - GC, :]
+            off = SC * (g % 2)
+            return grp[:, off + c0 : off + c1, :]
 
         def regroup(g, plan):
             for eng, c0, c1 in plan:
@@ -90,16 +86,15 @@ def tile_spectralchannelmixing_t_kernel(tc, x, wc, out):
                     else:
                         nc.scalar.copy(out=d4, in_=s4)
 
-        def quant(g, calls):
+        def quant(g, c0, c1):
             if g not in codes:
                 codes[g] = qx.tile([P, HW], U32, name="codes", align_bytes=64)
                 scales[g] = qx.tile([P, HW], U8, name="scales", align_bytes=64)
-            for c0, c1 in calls:
-                nc.vector.quantize_mx(
-                    out=codes[g][:, c0:c1].bitcast(FP8X4),
-                    scales=scales[g][:, c0:c1],
-                    in_=region(g, c0, c1).rearrange("p w t -> p (w t)"),
-                )
+            nc.vector.quantize_mx(
+                out=codes[g][:, c0:c1].bitcast(FP8X4),
+                scales=scales[g][:, c0:c1],
+                in_=region(g, c0, c1).rearrange("p w t -> p (w t)"),
+            )
 
         def w_regroup(i, eng):
             src = w_raw[i][:].rearrange("p t (q m) -> p m q t", m=PACK)
@@ -115,14 +110,16 @@ def tile_spectralchannelmixing_t_kernel(tc, x, wc, out):
                 in_=w_grp[i][:].rearrange("p m q t -> p (m q t)"),
             )
 
-        steady_plan = [("G", 0, GC), ("S", GC, HW)]
-        steady_calls = [(GC, HW), (0, HALF), (HALF, GC)]
+        def steady_plan(g):
+            if g % 2 == 0:
+                return [("G", SC, HW), ("S", 0, SC)]
+            return [("G", 0, HW - SC), ("S", HW - SC, HW)]
 
         w_regroup(0, "V")
         regroup(0, [("S", 0, 256), ("V", 256, HALF)])
         w_quant(0)
-        quant(0, [(0, HALF)])
-        regroup(0, [("G", HALF, GC), ("S", GC, HW)])
+        quant(0, 0, HALF)
+        regroup(0, [("G", HALF, 768), ("S", 768, HW)])
         w_regroup(1, "S")
 
         for g in range(NG):
@@ -150,15 +147,12 @@ def tile_spectralchannelmixing_t_kernel(tc, x, wc, out):
                         nc.scalar.activation(out=s[:, :, cols], in_=s[:, :, cols], func=GELU)
                         if h == 1:
                             nc.sync.dma_start(out=o_v[b, i], in_=s[:])
-                elif g < FINE:
+                elif g < NG - 1:
                     if h == 1:
                         nc.scalar.activation(out=s[:, m, :], in_=s[:, m, :], func=GELU)
-                        if g < WHOLE:
-                            if m == PACK - 1:
-                                nc.sync.dma_start(out=o_v[b, i], in_=s[:])
-                        elif m % 2 == 1:
+                        if m % 2 == 1:
                             nc.sync.dma_start(out=o_v[b, i][:, m - 1 : m + 1, :], in_=s[:, m - 1 : m + 1, :])
-                elif g < NG - 1 or m < PACK - 1:
+                elif m < PACK - 1:
                     if h == 1:
                         nc.scalar.activation(out=s[:, m, :], in_=s[:, m, :], func=GELU)
                         nc.sync.dma_start(out=o_v[b, i][:, m, :], in_=s[:, m, :])
@@ -167,14 +161,12 @@ def tile_spectralchannelmixing_t_kernel(tc, x, wc, out):
                     nc.sync.dma_start(out=o_v[b, i][:, m, cols], in_=s[:, m, cols])
 
                 if g == 0 and n == 1:
-                    quant(0, [(GC, HW), (HALF, GC)])
-                    regroup(1, [("G", 0, HALF), ("S", HALF, GC), ("S", GC, HW)])
-                elif g == 0 and n == 5:
-                    w_quant(1)
-                    quant(1, steady_calls)
-                    regroup(2, steady_plan)
-                elif g >= 1 and n == QPOS:
+                    quant(0, HALF, HW)
+                    regroup(1, [("G", 0, HALF), ("S", HALF, HW)])
+                elif n == QPOS:
+                    if g == 0:
+                        w_quant(1)
                     if g + 1 < NG:
-                        quant(g + 1, steady_calls)
+                        quant(g + 1, 0, HW)
                     if g + 2 < NG:
-                        regroup(g + 2, steady_plan)
+                        regroup(g + 2, steady_plan(g + 2))

@@ -20,9 +20,10 @@ HALF = 512
 NB = 4
 NI = 2
 NG = NB * NI
-SC = 256
+GC = 768
 QPOS = 5
 NSUM = 5
+WHOLE = 4
 
 
 def tile_spectralchannelmixing_t_kernel(tc, x, wc, out):
@@ -58,13 +59,15 @@ def tile_spectralchannelmixing_t_kernel(tc, x, wc, out):
         w_grp = [keep.tile([P, PACK, P, PACK], BF16, name="w_grp%d" % i, align_bytes=64) for i in range(NI)]
         w_codes = [keep.tile([P, 512], U32, name="w_codes%d" % i, align_bytes=64) for i in range(NI)]
         w_scales = [keep.tile([P, 512], U8, name="w_scales%d" % i, align_bytes=64) for i in range(NI)]
-        grp = keep.tile([P, HW + SC, PACK], BF16, name="grp", align_bytes=64)
+        g_big = keep.tile([P, GC, PACK], BF16, name="g_big", align_bytes=64)
+        g_small = [keep.tile([P, HW - GC, PACK], BF16, name="g_small%d" % k, align_bytes=64) for k in range(2)]
         codes = {}
         scales = {}
 
         def region(g, c0, c1):
-            off = SC * (g % 2)
-            return grp[:, off + c0 : off + c1, :]
+            if c1 <= GC:
+                return g_big[:, c0:c1, :]
+            return g_small[g % 2][:, c0 - GC : c1 - GC, :]
 
         def regroup(g, plan):
             for eng, c0, c1 in plan:
@@ -86,15 +89,16 @@ def tile_spectralchannelmixing_t_kernel(tc, x, wc, out):
                     else:
                         nc.scalar.copy(out=d4, in_=s4)
 
-        def quant(g, c0, c1):
+        def quant(g, calls):
             if g not in codes:
                 codes[g] = qx.tile([P, HW], U32, name="codes", align_bytes=64)
                 scales[g] = qx.tile([P, HW], U8, name="scales", align_bytes=64)
-            nc.vector.quantize_mx(
-                out=codes[g][:, c0:c1].bitcast(FP8X4),
-                scales=scales[g][:, c0:c1],
-                in_=region(g, c0, c1).rearrange("p w t -> p (w t)"),
-            )
+            for c0, c1 in calls:
+                nc.vector.quantize_mx(
+                    out=codes[g][:, c0:c1].bitcast(FP8X4),
+                    scales=scales[g][:, c0:c1],
+                    in_=region(g, c0, c1).rearrange("p w t -> p (w t)"),
+                )
 
         def w_regroup(i, eng):
             src = w_raw[i][:].rearrange("p t (q m) -> p m q t", m=PACK)
@@ -110,16 +114,21 @@ def tile_spectralchannelmixing_t_kernel(tc, x, wc, out):
                 in_=w_grp[i][:].rearrange("p m q t -> p (m q t)"),
             )
 
-        def steady_plan(g):
-            if g % 2 == 0:
-                return [("G", SC, HW), ("S", 0, SC)]
-            return [("G", 0, HW - SC), ("S", HW - SC, HW)]
+        steady_plan = [("G", 0, GC), ("S", GC, HW)]
+        steady_calls = [(GC, HW), (0, HALF), (HALF, GC)]
+
+        def cuts(g):
+            if g < WHOLE:
+                return [(0, 4)]
+            if g < NG - 1:
+                return [(0, 2), (2, 4)]
+            return [(0, 2), (2, 3), (3, 4)]
 
         w_regroup(0, "V")
         regroup(0, [("S", 0, 256), ("V", 256, HALF)])
         w_quant(0)
-        quant(0, 0, HALF)
-        regroup(0, [("G", HALF, 768), ("S", 768, HW)])
+        quant(0, [(0, HALF)])
+        regroup(0, [("G", HALF, GC), ("S", GC, HW)])
         w_regroup(1, "S")
 
         for g in range(NG):
@@ -147,26 +156,21 @@ def tile_spectralchannelmixing_t_kernel(tc, x, wc, out):
                         nc.scalar.activation(out=s[:, :, cols], in_=s[:, :, cols], func=GELU)
                         if h == 1:
                             nc.sync.dma_start(out=o_v[b, i], in_=s[:])
-                elif g < NG - 1:
-                    if h == 1:
-                        nc.scalar.activation(out=s[:, m, :], in_=s[:, m, :], func=GELU)
-                        if m % 2 == 1:
-                            nc.sync.dma_start(out=o_v[b, i][:, m - 1 : m + 1, :], in_=s[:, m - 1 : m + 1, :])
-                elif m < PACK - 1:
-                    if h == 1:
-                        nc.scalar.activation(out=s[:, m, :], in_=s[:, m, :], func=GELU)
-                        nc.sync.dma_start(out=o_v[b, i][:, m, :], in_=s[:, m, :])
-                else:
-                    nc.scalar.activation(out=s[:, m, cols], in_=s[:, m, cols], func=GELU)
-                    nc.sync.dma_start(out=o_v[b, i][:, m, cols], in_=s[:, m, cols])
+                elif h == 1:
+                    nc.scalar.activation(out=s[:, m, :], in_=s[:, m, :], func=GELU)
+                    for m0, m1 in cuts(g):
+                        if m1 == m + 1:
+                            nc.sync.dma_start(out=o_v[b, i][:, m0:m1, :], in_=s[:, m0:m1, :])
 
                 if g == 0 and n == 1:
-                    quant(0, HALF, HW)
-                    regroup(1, [("G", 0, HALF), ("S", HALF, HW)])
-                elif n == QPOS:
-                    if g == 0:
-                        w_quant(1)
+                    quant(0, [(GC, HW), (HALF, GC)])
+                    regroup(1, [("G", 0, HALF), ("S", HALF, GC), ("S", GC, HW)])
+                elif g == 0 and n == 5:
+                    w_quant(1)
+                    quant(1, steady_calls)
+                    regroup(2, steady_plan)
+                elif g >= 1 and n == QPOS:
                     if g + 1 < NG:
-                        quant(g + 1, 0, HW)
+                        quant(g + 1, steady_calls)
                     if g + 2 < NG:
-                        regroup(g + 2, steady_plan(g + 2))
+                        regroup(g + 2, steady_plan)

@@ -23,7 +23,6 @@ NG = NB * NI
 GC = 768
 QPOS = 5
 NSUM = 5
-WHOLE = 4
 
 
 def tile_spectralchannelmixing_t_kernel(tc, x, wc, out):
@@ -100,12 +99,12 @@ def tile_spectralchannelmixing_t_kernel(tc, x, wc, out):
                     in_=region(g, c0, c1).rearrange("p w t -> p (w t)"),
                 )
 
-        def w_regroup(i, eng):
-            src = w_raw[i][:].rearrange("p t (q m) -> p m q t", m=PACK)
+        def w_regroup(i, eng, m0, m1):
+            src = w_raw[i][:].rearrange("p t (q m) -> p m q t", m=PACK)[:, m0:m1, :, :]
             if eng == "V":
-                nc.vector.tensor_copy(out=w_grp[i][:], in_=src)
+                nc.vector.tensor_copy(out=w_grp[i][:, m0:m1, :, :], in_=src)
             else:
-                nc.scalar.copy(out=w_grp[i][:], in_=src)
+                nc.scalar.copy(out=w_grp[i][:, m0:m1, :, :], in_=src)
 
         def w_quant(i):
             nc.vector.quantize_mx(
@@ -117,19 +116,13 @@ def tile_spectralchannelmixing_t_kernel(tc, x, wc, out):
         steady_plan = [("G", 0, GC), ("S", GC, HW)]
         steady_calls = [(GC, HW), (0, HALF), (HALF, GC)]
 
-        def cuts(g):
-            if g < WHOLE:
-                return [(0, 4)]
-            if g < NG - 1:
-                return [(0, 2), (2, 4)]
-            return [(0, 2), (2, 3), (3, 4)]
-
-        w_regroup(0, "V")
-        regroup(0, [("S", 0, 256), ("V", 256, HALF)])
+        w_regroup(0, "V", 0, 3)
+        w_regroup(0, "S", 3, 4)
         w_quant(0)
+        regroup(0, [("S", 0, 256), ("V", 256, HALF)])
         quant(0, [(0, HALF)])
         regroup(0, [("G", HALF, GC), ("S", GC, HW)])
-        w_regroup(1, "S")
+        w_regroup(1, "S", 0, 4)
 
         for g in range(NG):
             b, i = bi(g)
@@ -150,17 +143,33 @@ def tile_spectralchannelmixing_t_kernel(tc, x, wc, out):
                     start=True,
                     stop=True,
                 )
+                if n == 7 and g == NG - 1:
+                    for c0 in (0, HALF // 2):
+                        qc = slice(HALF + c0, HALF + c0 + HALF // 2)
+                        nc.vector.tensor_tensor(
+                            out=s[:, m, qc], in0=acc[:, c0 : c0 + HALF // 2], in1=xs[g][:, m, qc], op=ADD
+                        )
+                        nc.scalar.activation(out=s[:, m, qc], in_=s[:, m, qc], func=GELU)
+                        nc.sync.dma_start(out=o_v[b, i][:, m, qc], in_=s[:, m, qc])
+                    continue
                 nc.vector.tensor_tensor(out=s[:, m, cols], in0=acc[:], in1=xs[g][:, m, cols], op=ADD)
                 if g == 0:
                     if m == PACK - 1:
                         nc.scalar.activation(out=s[:, :, cols], in_=s[:, :, cols], func=GELU)
                         if h == 1:
                             nc.sync.dma_start(out=o_v[b, i], in_=s[:])
-                elif h == 1:
-                    nc.scalar.activation(out=s[:, m, :], in_=s[:, m, :], func=GELU)
-                    for m0, m1 in cuts(g):
-                        if m1 == m + 1:
-                            nc.sync.dma_start(out=o_v[b, i][:, m0:m1, :], in_=s[:, m0:m1, :])
+                elif g < NG - 1:
+                    if h == 1:
+                        nc.scalar.activation(out=s[:, m, :], in_=s[:, m, :], func=GELU)
+                        if m % 2 == 1:
+                            nc.sync.dma_start(out=o_v[b, i][:, m - 1 : m + 1, :], in_=s[:, m - 1 : m + 1, :])
+                elif m < PACK - 1:
+                    if h == 1:
+                        nc.scalar.activation(out=s[:, m, :], in_=s[:, m, :], func=GELU)
+                        nc.sync.dma_start(out=o_v[b, i][:, m, :], in_=s[:, m, :])
+                else:
+                    nc.scalar.activation(out=s[:, m, cols], in_=s[:, m, cols], func=GELU)
+                    nc.sync.dma_start(out=o_v[b, i][:, m, cols], in_=s[:, m, cols])
 
                 if g == 0 and n == 1:
                     quant(0, [(GC, HW), (HALF, GC)])

@@ -36,7 +36,6 @@ def tile_spectralchannelmixing_t_kernel(tc, x, wc, out):
         qx = ctx.enter_context(tc.tile_pool(name="qx", bufs=2))
         sums = ctx.enter_context(tc.tile_pool(name="sums", bufs=NSUM))
         psum = ctx.enter_context(tc.psum_pool(name="psum", bufs=8))
-        ctx.enter_context(tc.manual_schedule())
 
         def bi(g):
             return g % NB, g // NB
@@ -99,12 +98,12 @@ def tile_spectralchannelmixing_t_kernel(tc, x, wc, out):
                     in_=region(g, c0, c1).rearrange("p w t -> p (w t)"),
                 )
 
-        def w_regroup(i, eng, m0, m1):
-            src = w_raw[i][:].rearrange("p t (q m) -> p m q t", m=PACK)[:, m0:m1, :, :]
+        def w_regroup(i, eng):
+            src = w_raw[i][:].rearrange("p t (q m) -> p m q t", m=PACK)
             if eng == "V":
-                nc.vector.tensor_copy(out=w_grp[i][:, m0:m1, :, :], in_=src)
+                nc.vector.tensor_copy(out=w_grp[i][:], in_=src)
             else:
-                nc.scalar.copy(out=w_grp[i][:, m0:m1, :, :], in_=src)
+                nc.scalar.copy(out=w_grp[i][:], in_=src)
 
         def w_quant(i):
             nc.vector.quantize_mx(
@@ -116,13 +115,12 @@ def tile_spectralchannelmixing_t_kernel(tc, x, wc, out):
         steady_plan = [("G", 0, GC), ("S", GC, HW)]
         steady_calls = [(GC, HW), (0, HALF), (HALF, GC)]
 
-        w_regroup(0, "V", 0, 3)
-        w_regroup(0, "S", 3, 4)
-        w_quant(0)
+        w_regroup(0, "V")
         regroup(0, [("S", 0, 256), ("V", 256, HALF)])
+        w_quant(0)
         quant(0, [(0, HALF)])
         regroup(0, [("G", HALF, GC), ("S", GC, HW)])
-        w_regroup(1, "S", 0, 4)
+        w_regroup(1, "S")
 
         for g in range(NG):
             b, i = bi(g)
@@ -143,15 +141,6 @@ def tile_spectralchannelmixing_t_kernel(tc, x, wc, out):
                     start=True,
                     stop=True,
                 )
-                if n == 7 and g == NG - 1:
-                    for c0 in (0, HALF // 2):
-                        qc = slice(HALF + c0, HALF + c0 + HALF // 2)
-                        nc.vector.tensor_tensor(
-                            out=s[:, m, qc], in0=acc[:, c0 : c0 + HALF // 2], in1=xs[g][:, m, qc], op=ADD
-                        )
-                        nc.scalar.activation(out=s[:, m, qc], in_=s[:, m, qc], func=GELU)
-                        nc.sync.dma_start(out=o_v[b, i][:, m, qc], in_=s[:, m, qc])
-                    continue
                 nc.vector.tensor_tensor(out=s[:, m, cols], in0=acc[:], in1=xs[g][:, m, cols], op=ADD)
                 if g == 0:
                     if m == PACK - 1:

from contextlib import ExitStack

import concourse.mybir as mybir

FLOPS = 2 * 4 * 1024 * 2 * 512 * 512

BF16 = mybir.dt.bfloat16
F32 = mybir.dt.float32
U32 = mybir.dt.uint32
U8 = mybir.dt.uint8
FP8X4 = mybir.dt.float8_e4m3fn_x4
ADD = mybir.AluOpType.add
MULT = mybir.AluOpType.mult
GELU = mybir.ActivationFunctionType.Gelu

P = 128
PACK = 4
HW = 1024
HALF = 512
NB = 4
NI = 2
NG = NB * NI
GC = 768
QPOS = 5
NSUM = 5


def tile_spectralchannelmixing_t_kernel(tc, x, wc, out):
    nc = tc.nc
    x_v = x.rearrange("b (i p t) h w -> b i p t (h w)", i=NI, p=P, t=PACK)
    o_v = out.rearrange("b (i q m) h w -> b i q m (h w)", i=NI, q=P, m=PACK)
    w_v = wc.rearrange("i (p t) k -> i p t k", t=PACK)

    with ExitStack() as ctx:
        keep = ctx.enter_context(tc.tile_pool(name="keep", bufs=1))
        qx = ctx.enter_context(tc.tile_pool(name="qx", bufs=2))
        sums = ctx.enter_context(tc.tile_pool(name="sums", bufs=NSUM))
        psum = ctx.enter_context(tc.psum_pool(name="psum", bufs=8))

        def bi(g):
            return g % NB, g // NB

        warm = keep.tile([P, 1], F32, name="warm")
        nc.vector.memset(warm[:], 0.0)
        nc.scalar.activation(out=warm[:], in_=warm[:], func=GELU)

        w_raw = [keep.tile([P, PACK, 512], BF16, name="w_raw%d" % i) for i in range(NI)]
        xs = [keep.tile([P, PACK, HW], BF16, name="xs%d" % g) for g in range(NG)]
        nc.sync.dma_start(out=w_raw[0][:], in_=w_v[0])
        nc.sync.dma_start(out=xs[0][:, :, 0:HALF], in_=x_v[0, 0][:, :, 0:HALF])
        nc.sync.dma_start(out=xs[0][:, :, HALF:HW], in_=x_v[0, 0][:, :, HALF:HW])
        nc.sync.dma_start(out=w_raw[1][:], in_=w_v[1])
        for g in range(1, NG):
            b, i = bi(g)
            nc.sync.dma_start(out=xs[g][:], in_=x_v[b, i])

        w_grp = [keep.tile([P, PACK, P, PACK], BF16, name="w_grp%d" % i, align_bytes=64) for i in range(NI)]
        w_codes = [keep.tile([P, 512], U32, name="w_codes%d" % i, align_bytes=64) for i in range(NI)]
        w_scales = [keep.tile([P, 512], U8, name="w_scales%d" % i, align_bytes=64) for i in range(NI)]
        g_big = keep.tile([P, GC, PACK], BF16, name="g_big", align_bytes=64)
        g_small = [keep.tile([P, HW - GC, PACK], BF16, name="g_small%d" % k, align_bytes=64) for k in range(2)]
        codes = {}
        scales = {}

        def region(g, c0, c1):
            if c1 <= GC:
                return g_big[:, c0:c1, :]
            return g_small[g % 2][:, c0 - GC : c1 - GC, :]

        def regroup(g, plan):
            for eng, c0, c1 in plan:
                dst = region(g, c0, c1)
                if eng == "G":
                    nc.gpsimd.tensor_scalar(
                        out=dst,
                        in0=xs[g][:, :, c0:c1].rearrange("p t w -> p w t"),
                        scalar1=1.0,
                        scalar2=0.0,
                        op0=MULT,
                        op1=ADD,
                    )
                else:
                    d4 = dst.rearrange("p (c i) t -> p c t i", i=4)
                    s4 = xs[g][:, :, c0:c1].rearrange("p t (c i) -> p c t i", i=4)
                    if eng == "V":
                        nc.vector.tensor_copy(out=d4, in_=s4)
                    else:
                        nc.scalar.copy(out=d4, in_=s4)

        def quant(g, calls):
            if g not in codes:
                codes[g] = qx.tile([P, HW], U32, name="codes", align_bytes=64)
                scales[g] = qx.tile([P, HW], U8, name="scales", align_bytes=64)
            for c0, c1 in calls:
                nc.vector.quantize_mx(
                    out=codes[g][:, c0:c1].bitcast(FP8X4),
                    scales=scales[g][:, c0:c1],
                    in_=region(g, c0, c1).rearrange("p w t -> p (w t)"),
                )

        def w_regroup(i, eng):
            src = w_raw[i][:].rearrange("p t (q m) -> p m q t", m=PACK)
            if eng == "V":
                nc.vector.tensor_copy(out=w_grp[i][:], in_=src)
            else:
                nc.scalar.copy(out=w_grp[i][:], in_=src)

        def w_quant(i):
            nc.vector.quantize_mx(
                out=w_codes[i][:].bitcast(FP8X4),
                scales=w_scales[i][:],
                in_=w_grp[i][:].rearrange("p m q t -> p (m q t)"),
            )

        steady_plan = [("G", 0, GC), ("S", GC, HW)]
        steady_calls = [(GC, HW), (0, HALF), (HALF, GC)]

        w_regroup(0, "V")
        regroup(0, [("S", 0, 256), ("V", 256, HALF)])
        w_quant(0)
        quant(0, [(0, HALF)])
        regroup(0, [("G", HALF, GC), ("S", GC, HW)])
        w_regroup(1, "S")

        for g in range(NG):
            b, i = bi(g)
            s = sums.tile([P, PACK, HW], F32, name="s")
            if g == 0:
                order = [(m, h) for h in range(2) for m in range(PACK)]
            else:
                order = [(m, h) for m in range(PACK) for h in range(2)]
            for n, (m, h) in enumerate(order):
                cols = slice(h * HALF, (h + 1) * HALF)
                acc = psum.tile([P, HALF], F32, name="acc")
                nc.tensor.matmul_mx(
                    out=acc[:],
                    lhsT=w_codes[i][:, m * P : (m + 1) * P].bitcast(FP8X4),
                    lhsT_scale=w_scales[i][:, m * P : (m + 1) * P],
                    rhs=codes[g][:, cols].bitcast(FP8X4),
                    rhs_scale=scales[g][:, cols],
                    start=True,
                    stop=True,
                )
                nc.vector.tensor_tensor(out=s[:, m, cols], in0=acc[:], in1=xs[g][:, m, cols], op=ADD)
                if g == 0:
                    if m == PACK - 1:
                        nc.scalar.activation(out=s[:, :, cols], in_=s[:, :, cols], func=GELU)
                        if h == 1:
                            nc.sync.dma_start(out=o_v[b, i], in_=s[:])
                elif g < NG - 1:
                    if h == 1:
                        nc.scalar.activation(out=s[:, m, :], in_=s[:, m, :], func=GELU)
                        if m % 2 == 1:
                            nc.sync.dma_start(out=o_v[b, i][:, m - 1 : m + 1, :], in_=s[:, m - 1 : m + 1, :])
                elif m < PACK - 1:
                    if h == 1:
                        nc.scalar.activation(out=s[:, m, :], in_=s[:, m, :], func=GELU)
                        nc.sync.dma_start(out=o_v[b, i][:, m, :], in_=s[:, m, :])
                else:
                    nc.scalar.activation(out=s[:, m, cols], in_=s[:, m, cols], func=GELU)
                    nc.sync.dma_start(out=o_v[b, i][:, m, cols], in_=s[:, m, cols])

                if g == 0 and n == 1:
                    quant(0, [(GC, HW), (HALF, GC)])
                    regroup(1, [("G", 0, HALF), ("S", HALF, GC), ("S", GC, HW)])
                elif g == 0 and n == 5:
                    w_quant(1)
                    quant(1, steady_calls)
                    regroup(2, steady_plan)
                elif g >= 1 and n == QPOS:
                    if g + 1 < NG:
                        quant(g + 1, steady_calls)
                    if g + 2 < NG:
                        regroup(g + 2, steady_plan)
